import numpy as np
import ml_dtypes


def mxq(x, axis, fmt="e4m3"):
    dtype, down = {"e4m3": (ml_dtypes.float8_e4m3fn, 7), "e5m2": (ml_dtypes.float8_e5m2, 14)}[fmt]
    v = np.moveaxis(np.asarray(x, np.float32).astype(ml_dtypes.bfloat16).astype(np.float64), axis, -1)
    blocks = v.reshape(v.shape[:-1] + (-1, 32))
    amax = np.abs(blocks).max(-1, keepdims=True)
    byte = np.maximum(np.where(amax > 0, np.frexp(amax)[1] - 1 + 127, 0) - down, 1)
    scale = np.exp2(byte - 127.0)
    codes = (blocks / scale).astype(np.float32).astype(dtype).astype(np.float64)
    return np.moveaxis((codes * scale).reshape(v.shape), -1, axis)


WIDE = False


def mx_kscale(k):
    if not WIDE:
        return np.ones(k)
    levels = np.array([10, -10, 5, -5, 0])
    if k % 512:
        return np.exp2(np.random.permutation(np.resize(levels, k // 32))).repeat(32)
    a = np.empty((k // 512, 16))
    for p in range(k // 512):
        a[p, :8] = np.random.permutation(np.resize(levels, 8))
        for g in range(8):
            far = levels[np.abs(levels - a[p, g]) >= 10]
            a[p, g + 8] = far[np.random.randint(len(far))]
    return np.exp2(a.ravel()).repeat(32)


BF16 = ml_dtypes.bfloat16


def bf(x):
    return np.asarray(x, np.float32).astype(BF16)


def f64(x):
    return np.asarray(x).astype(np.float64)


B, S, DM, H, DH, QB = 1, 512, 512, 8, 128, 512
DI = H * DH
EPS_GN = 1e-5


def setup_inputs():
    s = mx_kscale(DI)
    h = np.random.standard_normal((B, S, H, DH)) * 0.15 + np.random.standard_normal((B, 1, H, 1)) * 0.15
    return {"h_attn": bf(h.reshape(B, S, DI)),
            "gn_w": bf((1.0 + 0.1 * np.random.standard_normal(DI)) * s),
            "gn_b": bf(0.1 * np.random.standard_normal(DI) * s),
            "W_out": bf(np.random.standard_normal((DM, DI)) / np.sqrt(DI) / s[None, :]),
            "x": bf(np.random.standard_normal((B, S, DM))),
            "skip_scale": bf(0.7 + 0.1 * np.random.standard_normal(1))}


def reference(h_attn, gn_w, gn_b, W_out, x, skip_scale):
    hg = f64(h_attn).reshape(B, S, H, DH)
    mu = hg.mean(axis=(1, 3), keepdims=True)
    var = hg.var(axis=(1, 3), keepdims=True)
    hg = (hg - mu) / np.sqrt(var + EPS_GN)
    h = hg.reshape(B, S, DI) * f64(gn_w) + f64(gn_b)
    return (mxq(h, 2, "e4m3") @ mxq(f64(W_out), 1, "e4m3").T) + f64(skip_scale) * f64(x)

@@ -1,0 +1,232 @@
+from contextlib import ExitStack
+
+import concourse.mybir as mybir
+from concourse.masks import make_identity
+
+FLOPS = 2 * 512 * 512 * 1024
+
+BF16 = mybir.dt.bfloat16
+F32 = mybir.dt.float32
+U32 = mybir.dt.uint32
+U8 = mybir.dt.uint8
+FP8X4 = mybir.dt.float8_e4m3fn_x4
+ALU = mybir.AluOpType
+ACT = mybir.ActivationFunctionType
+
+P = 128
+S = 512
+DM = 512
+ROWS = S // P
+PASSES = 2
+PAIRS = 4
+PASS_CH = 512
+QUADS = 4
+HEAD_CH = 128
+EPS_GN = 1e-5
+GROUP_SIZE = S * HEAD_CH
+W_BLOCKS = DM // P
+W_BANKS = 3
+HALF = S // 2
+SCALAR_PAIRS = 3
+
+
+def tile_mlstmblock_pb_s_kernel(tc, h_attn, gn_w, gn_b, W_out, x, skip_scale, out):
+    nc = tc.nc
+    h_rows = h_attn.flatten_outer_dims().rearrange("(p j) k -> p j k", j=ROWS)
+    x_rows = x.flatten_outer_dims().rearrange("(p j) m -> p j m", j=ROWS)
+    out_rows = out.flatten_outer_dims().rearrange("(p j) m -> p j m", j=ROWS)
+    w_rows = W_out.rearrange("(b p) k -> b p k", p=P)
+
+    with ExitStack() as ctx:
+        const = ctx.enter_context(tc.tile_pool(name="const", bufs=1))
+        data = ctx.enter_context(tc.tile_pool(name="data", bufs=1))
+        stat = ctx.enter_context(tc.tile_pool(name="stat", bufs=1))
+        psum = ctx.enter_context(tc.psum_pool(name="psum", bufs=1))
+        ctx.enter_context(tc.manual_schedule())
+
+        gn_src = const.tile([P, PASS_CH], BF16)
+        nc.vector.memset(gn_src[:], 0.0)
+        nc.scalar.dma_start(out=gn_src[0:PASSES, :], in_=gn_w.rearrange("(g w) -> g w", g=PASSES))
+        nc.scalar.dma_start(out=gn_src[2 * PASSES : 3 * PASSES, :], in_=gn_b.rearrange("(g w) -> g w", g=PASSES))
+        skip_bf = const.tile([P, 1], BF16)
+        nc.scalar.dma_start(out=skip_bf[:], in_=skip_scale.partition_broadcast(P))
+
+        hx = []
+        for g in range(PASSES):
+            hx_g = data.tile([P, ROWS, PASS_CH], BF16, name="hx%d" % g)
+            for c in range(2):
+                cols = slice(256 * c, 256 * (c + 1))
+                nc.sync.dma_start(out=hx_g[:, :, cols], in_=h_rows[:, :, PASS_CH * g + 256 * c : PASS_CH * g + 256 * (c + 1)])
+            hx.append(hx_g)
+        w_sb = []
+        for b in range(W_BLOCKS):
+            w_b = data.tile([P, PASSES * PASS_CH], BF16, name="w_sb%d" % b)
+            nc.sync.dma_start(out=w_b[:], in_=w_rows[b])
+            w_sb.append(w_b)
+        x_sb = data.tile([P, ROWS, DM], BF16)
+        nc.sync.dma_start(out=x_sb[:], in_=x_rows)
+
+        ident = const.tile([P, P], F32)
+        make_identity(nc, ident[:])
+        warm = const.tile([P, 1], F32)
+        nc.vector.memset(warm[:], 1.0)
+        warm_out = const.tile([P, 1], F32)
+        nc.scalar.activation(out=warm_out[:], in_=warm[:], func=ACT.Abs_reciprocal_sqrt)
+        averager = const.tile([P, P], F32)
+        nc.vector.memset(averager[:], 1.0 / GROUP_SIZE)
+
+        small = psum.tile([P, 512], F32, tag="small")
+        gn_t = small[:, 0 : 2 * P].rearrange("q (u r) -> q u r", u=2)
+        means = small[:, 384:400].rearrange("p (k g f) -> p k g f", k=2, f=4)
+
+        def transpose_pair(c):
+            h_t_c = psum.tile([P, S], F32, tag="h_t%d" % c, name="h_t%d" % c)
+            words = hx[c // 2][:].bitcast(F32)
+            for j in range(ROWS):
+                nc.tensor.transpose(h_t_c[:, P * j : P * (j + 1)], words[:, j, c % 2 : 2 * P : 2], ident[:])
+            return h_t_c
+
+        sums = stat.tile([P, 2, PAIRS, 8], F32)
+        junk_sq_s = stat.tile([P, 2 * SCALAR_PAIRS, ROWS, HEAD_CH], BF16)
+        junk_sq_v = stat.tile([P, 2 * (PAIRS - SCALAR_PAIRS), ROWS, HEAD_CH], F32)
+        junk_sum = stat.tile([P, 2 * PAIRS, ROWS, HEAD_CH], BF16)
+        gn_all = const.tile([P, 3, PASSES, 4], F32)
+        skip = const.tile([P, 1], F32)
+        h_t = [None] * PAIRS
+        for c in range(PAIRS):
+            heads = [hx[c // 2][:, :, HEAD_CH * (2 * (c % 2) + f) : HEAD_CH * (2 * (c % 2) + f + 1)] for f in range(2)]
+            for f in range(2):
+                nc.vector.tensor_scalar(
+                    out=junk_sum[:, 2 * c + f], in0=heads[f], scalar1=-1.0, scalar2=None,
+                    op0=ALU.mult, op1=ALU.add, accum_out=sums[:, 0, c, f : f + 1],
+                )
+            for f in range(2):
+                if c < SCALAR_PAIRS:
+                    nc.scalar.activation(
+                        out=junk_sq_s[:, 2 * c + f], in_=heads[f], func=ACT.Square,
+                        accum_out=sums[:, 1, c, f : f + 1],
+                    )
+                else:
+                    nc.vector.scalar_tensor_tensor(
+                        out=junk_sq_v[:, 2 * (c - SCALAR_PAIRS) + f], in0=heads[f], scalar=1.0, in1=heads[f],
+                        op0=ALU.mult, op1=ALU.mult, accum_out=sums[:, 1, c, f : f + 1],
+                    )
+            if c == 1:
+                for u in range(2):
+                    h_t[u] = transpose_pair(u)
+        for u in range(2):
+            nc.tensor.transpose(gn_t[:, u], gn_src[:].bitcast(F32)[:, u : 2 * P : 2], ident[:])
+        nc.vector.tensor_copy(
+            out=gn_all[:].rearrange("q a g (u e) -> q (a g) u e", e=2),
+            in_=small[:, 0 : 2 * P].bitcast(BF16).rearrange("q (u r e) -> q r u e", u=2, e=2)[:, 0 : 3 * PASSES],
+        )
+        nc.vector.tensor_copy(out=skip[:], in_=skip_bf[:])
+        gb = gn_all[:, 2]
+
+        w_grp = data.tile([P, PASSES, 4 * DM], BF16, align_bytes=64)
+        w_grp_words = w_grp[:].bitcast(F32).rearrange("q g (m u) -> q g m u", u=2)
+
+        w_t = [None] * W_BLOCKS
+
+        def transpose_w_block(b):
+            w_t[b] = psum.tile([P, PAIRS, P], F32, tag="w_t%d" % (b % W_BANKS), name="w_t%d" % b)
+            words = w_sb[b][:].bitcast(F32)
+            for c in range(PAIRS):
+                start = 2 * P * (c // 2) + c % 2
+                nc.tensor.transpose(w_t[b][:, c, :], words[:, start : 2 * P * (c // 2 + 1) : 2], ident[:])
+
+        def copy_w_block(b):
+            nc.scalar.copy(
+                out=w_grp_words[:, :, P * b : P * (b + 1), :],
+                in_=w_t[b][:].rearrange("q (g u) m -> q g m u", u=2),
+            )
+
+        transpose_w_block(0)
+        copy_w_block(0)
+        transpose_w_block(1)
+        copy_w_block(1)
+        transpose_w_block(2)
+
+        nc.tensor.matmul(out=small[:, 384:400].rearrange("p (k c f) -> p k c f", k=2, f=2), lhsT=averager[:], rhs=sums[:, :, :, 0:2], start=True, stop=True)
+        sq_mean = stat.tile([P, PASSES, 4], F32)
+        nc.scalar.activation(out=sq_mean[:], in_=means[:, 0], func=ACT.Square)
+        copy_w_block(2)
+        var_eps = stat.tile([P, PASSES, 4], F32)
+        nc.vector.scalar_tensor_tensor(
+            out=var_eps[:], in0=means[:, 1], scalar=EPS_GN, in1=sq_mean[:], op0=ALU.add, op1=ALU.subtract
+        )
+        rstd = stat.tile([P, PASSES, 4], F32)
+        nc.scalar.activation(out=rstd[:], in_=var_eps[:], func=ACT.Abs_reciprocal_sqrt)
+        transpose_w_block(3)
+        copy_w_block(3)
+        by_rstd = stat.tile([P, 2, PASSES, 4], F32)
+        for f in range(QUADS):
+            rows = slice(32 * f, 32 * (f + 1))
+            nc.vector.tensor_tensor(
+                out=gn_all[rows, 1], in0=gn_all[rows, 0],
+                in1=means[rows, 0, :, f].unsqueeze(2).to_broadcast([32, PASSES, 4]), op=ALU.mult,
+            )
+        for f in range(QUADS):
+            rows = slice(32 * f, 32 * (f + 1))
+            nc.vector.tensor_tensor(
+                out=by_rstd[rows], in0=gn_all[rows, 0:2],
+                in1=rstd[rows, :, f].unsqueeze(1).unsqueeze(3).to_broadcast([32, 2, PASSES, 4]), op=ALU.mult,
+            )
+        scale = by_rstd[:, 0]
+        shift = stat.tile([P, PASSES, 4], F32)
+        nc.vector.tensor_tensor(out=shift[:], in0=by_rstd[:, 1], in1=gb, op=ALU.add)
+
+        for c in range(PAIRS // PASSES, PAIRS):
+            h_t[c] = transpose_pair(c)
+        w_codes = data.tile([P, PASSES, DM], U32, align_bytes=64)
+        w_scales = data.tile([P, PASSES, DM], U8, align_bytes=64)
+        for g in range(PASSES):
+            nc.vector.quantize_mx(
+                out=w_codes[:, g, :].bitcast(FP8X4), scales=w_scales[:, g, :], in_=w_grp[:, g, :]
+            )
+
+        h_codes = data.tile([P, PASSES, S], U32, align_bytes=64)
+        h_scales = data.tile([P, PASSES, S], U8, align_bytes=64)
+        acc_bank = ("w_t0", "w_t1", "w_t2", "h_t0")
+        acc = [None] * ROWS
+        for g in range(PASSES):
+            h_norm = data.tile([P, 4, S], BF16, name="h_norm%d" % g)
+            h_grp = data.tile([P, S, 4], BF16, name="h_grp%d" % g, align_bytes=64)
+            for half in range(2):
+                cols = slice(HALF * half, HALF * (half + 1))
+                for u in range(2):
+                    c = 2 * g + u
+                    halves = h_t[c][:].bitcast(BF16).rearrange("q (n e) -> q n e", e=2)
+                    for e in range(2):
+                        nc.scalar.activation(
+                            out=h_norm[:, 2 * u + e, cols], in_=halves[:, cols, e], func=ACT.Identity,
+                            scale=scale[:, g, 2 * u + e : 2 * u + e + 1], bias=shift[:, g, 2 * u + e : 2 * u + e + 1],
+                        )
+                nc.vector.tensor_copy(
+                    out=h_grp[:, cols, :].rearrange("q (c i) t -> q c t i", i=4),
+                    in_=h_norm[:, :, cols].rearrange("q t (c i) -> q c t i", i=4),
+                )
+                nc.vector.quantize_mx(
+                    out=h_codes[:, g, cols].bitcast(FP8X4), scales=h_scales[:, g, cols],
+                    in_=h_grp[:, cols, :].rearrange("q n t -> q (n t)"),
+                )
+                for j in range(2 * half, 2 * half + 2):
+                    if g == 0:
+                        acc[j] = psum.tile([P, DM], F32, tag=acc_bank[j], name="acc%d" % j)
+                    nc.tensor.matmul_mx(
+                        out=acc[j][:],
+                        lhsT=h_codes[:, g, P * j : P * (j + 1)].bitcast(FP8X4),
+                        lhsT_scale=h_scales[:, g, P * j : P * (j + 1)],
+                        rhs=w_codes[:, g, :].bitcast(FP8X4),
+                        rhs_scale=w_scales[:, g, :],
+                        start=(g == 0),
+                        stop=(g == PASSES - 1),
+                    )
+
+        out_sb = data.tile([P, ROWS, DM], F32)
+        for j in range(ROWS):
+            nc.vector.scalar_tensor_tensor(
+                out=out_sb[:, j, :], in0=x_sb[:, j, :], scalar=skip[:, 0:1], in1=acc[j][:],
+                op0=ALU.mult, op1=ALU.add,
+            )
+            nc.sync.dma_start(out=out_rows[:, j, :], in_=out_sb[:, j, :])

@@ -18,16 +18,12 @@ S = 512
 DM = 512
 ROWS = S // P
 PASSES = 2
-PAIRS = 4
 PASS_CH = 512
 QUADS = 4
 HEAD_CH = 128
 EPS_GN = 1e-5
 GROUP_SIZE = S * HEAD_CH
-W_BLOCKS = DM // P
-W_BANKS = 3
 HALF = S // 2
-SCALAR_PAIRS = 3
 
 
 def tile_mlstmblock_pb_s_kernel(tc, h_attn, gn_w, gn_b, W_out, x, skip_scale, out):
@@ -35,7 +31,7 @@ def tile_mlstmblock_pb_s_kernel(tc, h_attn, gn_w, gn_b, W_out, x, skip_scale, ou
     h_rows = h_attn.flatten_outer_dims().rearrange("(p j) k -> p j k", j=ROWS)
     x_rows = x.flatten_outer_dims().rearrange("(p j) m -> p j m", j=ROWS)
     out_rows = out.flatten_outer_dims().rearrange("(p j) m -> p j m", j=ROWS)
-    w_rows = W_out.rearrange("(b p) k -> b p k", p=P)
+    w_rows = W_out.rearrange("(b p) k -> p b k", p=P)
 
     with ExitStack() as ctx:
         const = ctx.enter_context(tc.tile_pool(name="const", bufs=1))
@@ -46,187 +42,295 @@ def tile_mlstmblock_pb_s_kernel(tc, h_attn, gn_w, gn_b, W_out, x, skip_scale, ou
 
         gn_src = const.tile([P, PASS_CH], BF16)
         nc.vector.memset(gn_src[:], 0.0)
-        nc.scalar.dma_start(out=gn_src[0:PASSES, :], in_=gn_w.rearrange("(g w) -> g w", g=PASSES))
-        nc.scalar.dma_start(out=gn_src[2 * PASSES : 3 * PASSES, :], in_=gn_b.rearrange("(g w) -> g w", g=PASSES))
-        skip_bf = const.tile([P, 1], BF16)
-        nc.scalar.dma_start(out=skip_bf[:], in_=skip_scale.partition_broadcast(P))
-
         hx = []
         for g in range(PASSES):
             hx_g = data.tile([P, ROWS, PASS_CH], BF16, name="hx%d" % g)
+            hx.append(hx_g)
+        for g in range(PASSES):
             for c in range(2):
                 cols = slice(256 * c, 256 * (c + 1))
-                nc.sync.dma_start(out=hx_g[:, :, cols], in_=h_rows[:, :, PASS_CH * g + 256 * c : PASS_CH * g + 256 * (c + 1)])
-            hx.append(hx_g)
+                nc.sync.dma_start(out=hx[g][:, :, cols], in_=h_rows[:, :, PASS_CH * g + 256 * c : PASS_CH * g + 256 * (c + 1)])
+            if g == 0:
+                nc.sync.dma_start(out=gn_src[0:2, :], in_=gn_w.rearrange("(g w) -> g w", g=PASSES))
+                nc.sync.dma_start(out=gn_src[6:8, :], in_=gn_b.rearrange("(g w) -> g w", g=PASSES))
         w_sb = []
-        for b in range(W_BLOCKS):
-            w_b = data.tile([P, PASSES * PASS_CH], BF16, name="w_sb%d" % b)
-            nc.sync.dma_start(out=w_b[:], in_=w_rows[b])
-            w_sb.append(w_b)
+        for g in range(PASSES):
+            w_g = data.tile([P, 4, PASS_CH], BF16, name="w_sb%d" % g)
+            nc.sync.dma_start(out=w_g[:], in_=w_rows[:, :, PASS_CH * g : PASS_CH * (g + 1)])
+            w_sb.append(w_g)
         x_sb = data.tile([P, ROWS, DM], BF16)
         nc.sync.dma_start(out=x_sb[:], in_=x_rows)
+        skip_bf = const.tile([P, 1], BF16)
+        nc.sync.dma_start(out=skip_bf[:], in_=skip_scale.partition_broadcast(P))
 
-        ident = const.tile([P, P], F32)
-        make_identity(nc, ident[:])
         warm = const.tile([P, 1], F32)
         nc.vector.memset(warm[:], 1.0)
         warm_out = const.tile([P, 1], F32)
         nc.scalar.activation(out=warm_out[:], in_=warm[:], func=ACT.Abs_reciprocal_sqrt)
+        ident = const.tile([P, P], F32)
+        make_identity(nc, ident[:])
+        neg_ones = const.tile([P, 2], BF16)
+        nc.vector.memset(neg_ones[:], -1.0)
         averager = const.tile([P, P], F32)
         nc.vector.memset(averager[:], 1.0 / GROUP_SIZE)
 
         small = psum.tile([P, 512], F32, tag="small")
-        gn_t = small[:, 0 : 2 * P].rearrange("q (u r) -> q u r", u=2)
-        means = small[:, 384:400].rearrange("p (k g f) -> p k g f", k=2, f=4)
+        gn_bank = psum.tile([P, 512], F32, tag="w1", name="gn_bank")
+        gn_t = gn_bank[:, 0 : 2 * P].rearrange("q (u r) -> q u r", u=2)
+        stat_bank = (small, psum.tile([P, 512], F32, tag="small1", name="small1"))
+        means = [stat_bank[g][:, 32:48].rearrange("q (f k e) -> q f k e", f=QUADS, k=2) for g in range(PASSES)]
 
-        def transpose_pair(c):
-            h_t_c = psum.tile([P, S], F32, tag="h_t%d" % c, name="h_t%d" % c)
-            words = hx[c // 2][:].bitcast(F32)
+        h_t = [
+            [psum.tile([P, S], F32, tag="h_t%d%d" % (g, u), name="h_t%d%d" % (g, u)) for u in range(2)]
+            for g in range(PASSES)
+        ]
+
+        sums = stat.tile([P, PASSES, QUADS, 2, 2], F32)
+        nc.vector.memset(sums[:], 0.0)
+        junk_s = stat.tile([P, 8, ROWS, HEAD_CH], BF16)
+        bn = stat.tile([P, PASSES, QUADS, 2, 3], F32)
+        sq_mean = stat.tile([P, PASSES, QUADS, 2], F32)
+        heads_s = (slice(0, 4, 2), slice(0, 3))
+        heads_v = (slice(1, 4, 2), slice(3, 4))
+        sel = stat.tile([P, PASSES, 2], F32)
+        gn_all = const.tile([P, 4, PASSES, 4], F32)
+        negvar = stat.tile([P, PASSES], F32)
+        rstd = stat.tile([P, PASSES], F32)
+        ss = stat.tile([P, PASSES, 2, 4], F32)
+
+        def head(g, f):
+            return hx[g][:, :, HEAD_CH * f : HEAD_CH * (f + 1)]
+
+        def pe_sum(g, f):
             for j in range(ROWS):
-                nc.tensor.transpose(h_t_c[:, P * j : P * (j + 1)], words[:, j, c % 2 : 2 * P : 2], ident[:])
-            return h_t_c
-
-        sums = stat.tile([P, 2, PAIRS, 8], F32)
-        junk_sq_s = stat.tile([P, 2 * SCALAR_PAIRS, ROWS, HEAD_CH], BF16)
-        junk_sq_v = stat.tile([P, 2 * (PAIRS - SCALAR_PAIRS), ROWS, HEAD_CH], F32)
-        junk_sum = stat.tile([P, 2 * PAIRS, ROWS, HEAD_CH], BF16)
-        gn_all = const.tile([P, 3, PASSES, 4], F32)
-        skip = const.tile([P, 1], F32)
-        h_t = [None] * PAIRS
-        for c in range(PAIRS):
-            heads = [hx[c // 2][:, :, HEAD_CH * (2 * (c % 2) + f) : HEAD_CH * (2 * (c % 2) + f + 1)] for f in range(2)]
-            for f in range(2):
-                nc.vector.tensor_scalar(
-                    out=junk_sum[:, 2 * c + f], in0=heads[f], scalar1=-1.0, scalar2=None,
-                    op0=ALU.mult, op1=ALU.add, accum_out=sums[:, 0, c, f : f + 1],
+                nc.tensor.matmul(
+                    out=stat_bank[g][:, f : f + 1], lhsT=head(g, f)[:, j, :], rhs=neg_ones[:, 0:1],
+                    start=(j == 0), stop=(j == ROWS - 1),
                 )
-            for f in range(2):
-                if c < SCALAR_PAIRS:
-                    nc.scalar.activation(
-                        out=junk_sq_s[:, 2 * c + f], in_=heads[f], func=ACT.Square,
-                        accum_out=sums[:, 1, c, f : f + 1],
-                    )
-                else:
-                    nc.vector.scalar_tensor_tensor(
-                        out=junk_sq_v[:, 2 * (c - SCALAR_PAIRS) + f], in0=heads[f], scalar=1.0, in1=heads[f],
-                        op0=ALU.mult, op1=ALU.mult, accum_out=sums[:, 1, c, f : f + 1],
-                    )
-            if c == 1:
-                for u in range(2):
-                    h_t[u] = transpose_pair(u)
-        for u in range(2):
-            nc.tensor.transpose(gn_t[:, u], gn_src[:].bitcast(F32)[:, u : 2 * P : 2], ident[:])
-        nc.vector.tensor_copy(
-            out=gn_all[:].rearrange("q a g (u e) -> q (a g) u e", e=2),
-            in_=small[:, 0 : 2 * P].bitcast(BF16).rearrange("q (u r e) -> q r u e", u=2, e=2)[:, 0 : 3 * PASSES],
-        )
-        nc.vector.tensor_copy(out=skip[:], in_=skip_bf[:])
-        gb = gn_all[:, 2]
+
+        def s_square(g, f):
+            nc.scalar.activation(
+                out=junk_s[:, 4 * g + f], in_=head(g, f), func=ACT.Square, accum_out=sums[:, g, f, 1, 0:1]
+            )
+
+        def v_bn(g, f):
+            nc.vector.bn_stats(out=bn[:, g, f].rearrange("p e c -> p (e c)"), in_=head(g, f))
+
+        def v_copy_sums(g):
+            nc.vector.tensor_copy(out=sums[:, g, heads_s[g], 0, 0], in_=stat_bank[g][:, heads_s[g]])
+
+        def v_bn_post(g):
+            mean = bn[:, g, heads_v[g], :, 1]
+            nc.vector.scalar_tensor_tensor(
+                out=sq_mean[:, g, heads_v[g]], in0=mean, scalar=256.0, in1=mean, op0=ALU.mult, op1=ALU.mult
+            )
+            nc.vector.tensor_scalar(
+                out=sums[:, g, heads_v[g], 0, :], in0=mean, scalar1=-256.0, scalar2=None, op0=ALU.mult
+            )
+            nc.vector.tensor_tensor(
+                out=sums[:, g, heads_v[g], 1, :], in0=bn[:, g, heads_v[g], :, 2], in1=sq_mean[:, g, heads_v[g]], op=ALU.add
+            )
+
+        def pe_means(g):
+            nc.tensor.matmul(
+                out=stat_bank[g][:, 32:48], lhsT=averager[:], rhs=sums[:, g].rearrange("p f k e -> p (f k e)"),
+                start=True, stop=True,
+            )
+
+        def pe_h(g, u):
+            words = hx[g][:].bitcast(F32)
+            for j in range(ROWS):
+                nc.tensor.transpose(h_t[g][u][:, P * j : P * (j + 1)], words[:, j, u : 2 * P : 2], ident[:])
+
+        def v_var(g):
+            for f in range(QUADS):
+                rows = slice(32 * f, 32 * (f + 1))
+                nc.vector.tensor_reduce(
+                    out=sel[rows, g], in_=means[g][rows, f], axis=mybir.AxisListType.X, op=ALU.add
+                )
+            nc.vector.tensor_scalar(
+                out=negvar[:, g : g + 1], in0=sel[:, g, 0:1], scalar1=sel[:, g, 0:1], scalar2=sel[:, g, 1:2],
+                op0=ALU.mult, op1=ALU.subtract,
+            )
+            nc.vector.tensor_scalar(
+                out=gn_all[:, 1, g, :], in0=gn_all[:, 0, g, :], scalar1=sel[:, g, 0:1], scalar2=None, op0=ALU.mult
+            )
+
+        def s_rstd(g):
+            nc.scalar.activation(
+                out=rstd[:, g : g + 1], in_=negvar[:, g : g + 1], func=ACT.Abs_reciprocal_sqrt, scale=-1.0, bias=EPS_GN
+            )
+
+        def v_scale_shift(g):
+            nc.vector.scalar_tensor_tensor(
+                out=ss[:, g], in0=gn_all[:, 0:2, g, :], scalar=rstd[:, g : g + 1], in1=gn_all[:, 2:4, g, :],
+                op0=ALU.mult, op1=ALU.add,
+            )
 
         w_grp = data.tile([P, PASSES, 4 * DM], BF16, align_bytes=64)
-        w_grp_words = w_grp[:].bitcast(F32).rearrange("q g (m u) -> q g m u", u=2)
-
-        w_t = [None] * W_BLOCKS
-
-        def transpose_w_block(b):
-            w_t[b] = psum.tile([P, PAIRS, P], F32, tag="w_t%d" % (b % W_BANKS), name="w_t%d" % b)
-            words = w_sb[b][:].bitcast(F32)
-            for c in range(PAIRS):
-                start = 2 * P * (c // 2) + c % 2
-                nc.tensor.transpose(w_t[b][:, c, :], words[:, start : 2 * P * (c // 2 + 1) : 2], ident[:])
-
-        def copy_w_block(b):
-            nc.scalar.copy(
-                out=w_grp_words[:, :, P * b : P * (b + 1), :],
-                in_=w_t[b][:].rearrange("q (g u) m -> q g m u", u=2),
-            )
-
-        transpose_w_block(0)
-        copy_w_block(0)
-        transpose_w_block(1)
-        copy_w_block(1)
-        transpose_w_block(2)
-
-        nc.tensor.matmul(out=small[:, 384:400].rearrange("p (k c f) -> p k c f", k=2, f=2), lhsT=averager[:], rhs=sums[:, :, :, 0:2], start=True, stop=True)
-        sq_mean = stat.tile([P, PASSES, 4], F32)
-        nc.scalar.activation(out=sq_mean[:], in_=means[:, 0], func=ACT.Square)
-        copy_w_block(2)
-        var_eps = stat.tile([P, PASSES, 4], F32)
-        nc.vector.scalar_tensor_tensor(
-            out=var_eps[:], in0=means[:, 1], scalar=EPS_GN, in1=sq_mean[:], op0=ALU.add, op1=ALU.subtract
-        )
-        rstd = stat.tile([P, PASSES, 4], F32)
-        nc.scalar.activation(out=rstd[:], in_=var_eps[:], func=ACT.Abs_reciprocal_sqrt)
-        transpose_w_block(3)
-        copy_w_block(3)
-        by_rstd = stat.tile([P, 2, PASSES, 4], F32)
-        for f in range(QUADS):
-            rows = slice(32 * f, 32 * (f + 1))
-            nc.vector.tensor_tensor(
-                out=gn_all[rows, 1], in0=gn_all[rows, 0],
-                in1=means[rows, 0, :, f].unsqueeze(2).to_broadcast([32, PASSES, 4]), op=ALU.mult,
-            )
-        for f in range(QUADS):
-            rows = slice(32 * f, 32 * (f + 1))
-            nc.vector.tensor_tensor(
-                out=by_rstd[rows], in0=gn_all[rows, 0:2],
-                in1=rstd[rows, :, f].unsqueeze(1).unsqueeze(3).to_broadcast([32, 2, PASSES, 4]), op=ALU.mult,
-            )
-        scale = by_rstd[:, 0]
-        shift = stat.tile([P, PASSES, 4], F32)
-        nc.vector.tensor_tensor(out=shift[:], in0=by_rstd[:, 1], in1=gb, op=ALU.add)
-
-        for c in range(PAIRS // PASSES, PAIRS):
-            h_t[c] = transpose_pair(c)
+        w_words = w_grp[:].bitcast(F32).rearrange("q g (m u) -> q g m u", u=2)
         w_codes = data.tile([P, PASSES, DM], U32, align_bytes=64)
         w_scales = data.tile([P, PASSES, DM], U8, align_bytes=64)
-        for g in range(PASSES):
+        w_t = {}
+        w_bank = (("w0", "w1"), ("small", "small1"))
+
+        def pe_w(g, bp):
+            w_t[(g, bp)] = psum.tile([P, 2, 256], F32, tag=w_bank[g][bp], name="w_t%d%d" % (g, bp))
+            words = w_sb[g][:].bitcast(F32)
+            for b in range(2):
+                for u in range(2):
+                    nc.tensor.transpose(
+                        w_t[(g, bp)][:, u, P * b : P * (b + 1)], words[:, 2 * bp + b, u : 2 * P : 2], ident[:]
+                    )
+
+        def s_copy_w(g, bp):
+            nc.scalar.copy(
+                out=w_words[:, g, 256 * bp : 256 * (bp + 1), :], in_=w_t[(g, bp)][:].rearrange("q u m -> q m u")
+            )
+
+        def v_quant_w(g):
             nc.vector.quantize_mx(
                 out=w_codes[:, g, :].bitcast(FP8X4), scales=w_scales[:, g, :], in_=w_grp[:, g, :]
             )
 
+        h_norm = [data.tile([P, 4, S], BF16, name="h_norm%d" % g) for g in range(PASSES)]
+        h_grp = [data.tile([P, S, 4], BF16, name="h_grp%d" % g, align_bytes=64) for g in range(PASSES)]
         h_codes = data.tile([P, PASSES, S], U32, align_bytes=64)
         h_scales = data.tile([P, PASSES, S], U8, align_bytes=64)
-        acc_bank = ("w_t0", "w_t1", "w_t2", "h_t0")
-        acc = [None] * ROWS
-        for g in range(PASSES):
-            h_norm = data.tile([P, 4, S], BF16, name="h_norm%d" % g)
-            h_grp = data.tile([P, S, 4], BF16, name="h_grp%d" % g, align_bytes=64)
-            for half in range(2):
-                cols = slice(HALF * half, HALF * (half + 1))
-                for u in range(2):
-                    c = 2 * g + u
-                    halves = h_t[c][:].bitcast(BF16).rearrange("q (n e) -> q n e", e=2)
-                    for e in range(2):
-                        nc.scalar.activation(
-                            out=h_norm[:, 2 * u + e, cols], in_=halves[:, cols, e], func=ACT.Identity,
-                            scale=scale[:, g, 2 * u + e : 2 * u + e + 1], bias=shift[:, g, 2 * u + e : 2 * u + e + 1],
-                        )
-                nc.vector.tensor_copy(
-                    out=h_grp[:, cols, :].rearrange("q (c i) t -> q c t i", i=4),
-                    in_=h_norm[:, :, cols].rearrange("q t (c i) -> q c t i", i=4),
+
+        def half_cols(half):
+            return slice(HALF * half, HALF * (half + 1))
+
+        def h_t_values(g, t):
+            return h_t[g][t // 2][:].bitcast(BF16).rearrange("q (n e) -> q n e", e=2)[:, :, t % 2]
+
+        def s_norm(g, half, t):
+            nc.scalar.activation(
+                out=h_norm[g][:, t, half_cols(half)], in_=h_t_values(g, t)[:, half_cols(half)],
+                func=ACT.Identity, scale=ss[:, g, 0, t : t + 1], bias=ss[:, g, 1, t : t + 1],
+            )
+
+        def v_norm(g, half, t):
+            nc.vector.tensor_scalar(
+                out=h_norm[g][:, t, half_cols(half)], in0=h_t_values(g, t)[:, half_cols(half)],
+                scalar1=ss[:, g, 0, t : t + 1], scalar2=ss[:, g, 1, t : t + 1], op0=ALU.mult, op1=ALU.add,
+            )
+
+        def v_group(g, half):
+            cols = half_cols(half)
+            nc.vector.tensor_copy(
+                out=h_grp[g][:, cols, :].rearrange("q (c i) t -> q c t i", i=4),
+                in_=h_norm[g][:, :, cols].rearrange("q t (c i) -> q c t i", i=4),
+            )
+
+        def v_quant_h(g, half):
+            cols = half_cols(half)
+            nc.vector.quantize_mx(
+                out=h_codes[:, g, cols].bitcast(FP8X4), scales=h_scales[:, g, cols],
+                in_=h_grp[g][:, cols, :].rearrange("q n t -> q (n t)"),
+            )
+
+        acc_bank = ("w0", "w1", "small", "small1")
+        acc = {}
+
+        def pe_mx(g, half):
+            for j in range(2 * half, 2 * half + 2):
+                if g == 0:
+                    acc[j] = psum.tile([P, DM], F32, tag=acc_bank[j], name="acc%d" % j)
+                nc.tensor.matmul_mx(
+                    out=acc[j][:],
+                    lhsT=h_codes[:, g, P * j : P * (j + 1)].bitcast(FP8X4),
+                    lhsT_scale=h_scales[:, g, P * j : P * (j + 1)],
+                    rhs=w_codes[:, g, :].bitcast(FP8X4),
+                    rhs_scale=w_scales[:, g, :],
+                    start=(g == 0),
+                    stop=(g == PASSES - 1),
                 )
-                nc.vector.quantize_mx(
-                    out=h_codes[:, g, cols].bitcast(FP8X4), scales=h_scales[:, g, cols],
-                    in_=h_grp[:, cols, :].rearrange("q n t -> q (n t)"),
-                )
-                for j in range(2 * half, 2 * half + 2):
-                    if g == 0:
-                        acc[j] = psum.tile([P, DM], F32, tag=acc_bank[j], name="acc%d" % j)
-                    nc.tensor.matmul_mx(
-                        out=acc[j][:],
-                        lhsT=h_codes[:, g, P * j : P * (j + 1)].bitcast(FP8X4),
-                        lhsT_scale=h_scales[:, g, P * j : P * (j + 1)],
-                        rhs=w_codes[:, g, :].bitcast(FP8X4),
-                        rhs_scale=w_scales[:, g, :],
-                        start=(g == 0),
-                        stop=(g == PASSES - 1),
-                    )
 
         out_sb = data.tile([P, ROWS, DM], F32)
-        for j in range(ROWS):
+        skip = const.tile([P, 1], F32)
+
+        def v_out(j):
             nc.vector.scalar_tensor_tensor(
-                out=out_sb[:, j, :], in0=x_sb[:, j, :], scalar=skip[:, 0:1], in1=acc[j][:],
-                op0=ALU.mult, op1=ALU.add,
+                out=out_sb[:, j, :], in0=x_sb[:, j, :], scalar=skip[:, 0:1], in1=acc[j][:], op0=ALU.mult, op1=ALU.add
             )
             nc.sync.dma_start(out=out_rows[:, j, :], in_=out_sb[:, j, :])
+
+        s_square(0, 0)
+        v_bn(0, 1)
+        s_square(0, 2)
+        v_bn(0, 3)
+        pe_sum(0, 0)
+        pe_sum(0, 2)
+        for u in range(2):
+            nc.tensor.transpose(gn_t[:, u], gn_src[:].bitcast(F32)[:, u : 2 * P : 2], ident[:])
+        v_copy_sums(0)
+        v_bn_post(0)
+        pe_h(0, 0)
+        pe_means(0)
+        s_square(1, 0)
+        pe_sum(1, 0)
+        s_square(1, 1)
+        pe_sum(1, 1)
+        s_square(1, 2)
+        pe_sum(1, 2)
+        nc.vector.tensor_copy(
+            out=gn_all[:].rearrange("q a g (u e) -> q (a g) u e", e=2),
+            in_=gn_bank[:, 0 : 2 * P].bitcast(BF16).rearrange("q (u r e) -> q r u e", u=2, e=2)[:, 0:8],
+        )
+        v_bn(1, 3)
+        pe_h(0, 1)
+        v_var(0)
+        s_rstd(0)
+        v_bn_post(1)
+        v_copy_sums(1)
+        pe_means(1)
+        v_scale_shift(0)
+        s_norm(0, 0, 0)
+        s_norm(0, 0, 1)
+        v_norm(0, 0, 2)
+        v_norm(0, 0, 3)
+        pe_w(0, 0)
+        pe_w(0, 1)
+        v_var(1)
+        s_norm(0, 1, 0)
+        s_norm(0, 1, 1)
+        s_rstd(1)
+        s_norm(0, 1, 2)
+        s_norm(0, 1, 3)
+        v_group(0, 0)
+        v_scale_shift(1)
+        s_copy_w(0, 0)
+        v_quant_h(0, 0)
+        v_group(0, 1)
+        s_copy_w(0, 1)
+        pe_h(1, 0)
+        pe_h(1, 1)
+        pe_w(1, 0)
+        pe_w(1, 1)
+        v_quant_h(0, 1)
+        s_norm(1, 0, 0)
+        s_norm(1, 0, 1)
+        v_quant_w(0)
+        s_copy_w(1, 0)
+        s_norm(1, 0, 2)
+        s_norm(1, 0, 3)
+        s_copy_w(1, 1)
+        pe_mx(0, 0)
+        pe_mx(0, 1)
+        v_group(1, 0)
+        s_norm(1, 1, 0)
+        s_norm(1, 1, 1)
+        s_norm(1, 1, 2)
+        s_norm(1, 1, 3)
+        v_quant_h(1, 0)
+        v_quant_w(1)
+        pe_mx(1, 0)
+        v_group(1, 1)
+        nc.vector.tensor_copy(out=skip[:], in_=skip_bf[:])
+        v_out(0)
+        v_quant_h(1, 1)
+        pe_mx(1, 1)
+        v_out(1)
+        v_out(2)
+        v_out(3)

@@ -78,20 +78,16 @@ def tile_mlstmblock_pb_s_kernel(tc, h_attn, gn_w, gn_b, W_out, x, skip_scale, ou
         gn_bank = psum.tile([P, 512], F32, tag="w1", name="gn_bank")
         gn_t = gn_bank[:, 0 : 2 * P].rearrange("q (u r) -> q u r", u=2)
         stat_bank = (small, psum.tile([P, 512], F32, tag="small1", name="small1"))
-        means = [stat_bank[g][:, 32:48].rearrange("q (f k e) -> q f k e", f=QUADS, k=2) for g in range(PASSES)]
+        means = [stat_bank[g][:, 32:40].rearrange("q (f k) -> q f k", f=QUADS) for g in range(PASSES)]
 
         h_t = [
             [psum.tile([P, S], F32, tag="h_t%d%d" % (g, u), name="h_t%d%d" % (g, u)) for u in range(2)]
             for g in range(PASSES)
         ]
 
-        sums = stat.tile([P, PASSES, QUADS, 2, 2], F32)
-        nc.vector.memset(sums[:], 0.0)
+        sums = stat.tile([P, PASSES, QUADS, 2], F32)
         junk_s = stat.tile([P, 8, ROWS, HEAD_CH], BF16)
-        bn = stat.tile([P, PASSES, QUADS, 2, 3], F32)
-        sq_mean = stat.tile([P, PASSES, QUADS, 2], F32)
-        heads_s = (slice(0, 4, 2), slice(0, 3))
-        heads_v = (slice(1, 4, 2), slice(3, 4))
+        junk_v = stat.tile([P, 8, ROWS, HEAD_CH], BF16)
         sel = stat.tile([P, PASSES, 2], F32)
         gn_all = const.tile([P, 4, PASSES, 4], F32)
         negvar = stat.tile([P, PASSES], F32)
@@ -110,30 +106,21 @@ def tile_mlstmblock_pb_s_kernel(tc, h_attn, gn_w, gn_b, W_out, x, skip_scale, ou
 
         def s_square(g, f):
             nc.scalar.activation(
-                out=junk_s[:, 4 * g + f], in_=head(g, f), func=ACT.Square, accum_out=sums[:, g, f, 1, 0:1]
+                out=junk_s[:, 4 * g + f], in_=head(g, f), func=ACT.Square, accum_out=sums[:, g, f, 1:2]
             )
 
         def v_bn(g, f):
-            nc.vector.bn_stats(out=bn[:, g, f].rearrange("p e c -> p (e c)"), in_=head(g, f))
+            nc.vector.scalar_tensor_tensor(
+                out=junk_v[:, 4 * g + f], in0=head(g, f), scalar=1.0, in1=head(g, f), op0=ALU.mult, op1=ALU.mult,
+                accum_out=sums[:, g, f, 1:2],
+            )
 
         def v_copy_sums(g):
-            nc.vector.tensor_copy(out=sums[:, g, heads_s[g], 0, 0], in_=stat_bank[g][:, heads_s[g]])
-
-        def v_bn_post(g):
-            mean = bn[:, g, heads_v[g], :, 1]
-            nc.vector.scalar_tensor_tensor(
-                out=sq_mean[:, g, heads_v[g]], in0=mean, scalar=256.0, in1=mean, op0=ALU.mult, op1=ALU.mult
-            )
-            nc.vector.tensor_scalar(
-                out=sums[:, g, heads_v[g], 0, :], in0=mean, scalar1=-256.0, scalar2=None, op0=ALU.mult
-            )
-            nc.vector.tensor_tensor(
-                out=sums[:, g, heads_v[g], 1, :], in0=bn[:, g, heads_v[g], :, 2], in1=sq_mean[:, g, heads_v[g]], op=ALU.add
-            )
+            nc.vector.tensor_copy(out=sums[:, g, :, 0], in_=stat_bank[g][:, 0:QUADS])
 
         def pe_means(g):
             nc.tensor.matmul(
-                out=stat_bank[g][:, 32:48], lhsT=averager[:], rhs=sums[:, g].rearrange("p f k e -> p (f k e)"),
+                out=stat_bank[g][:, 32:40], lhsT=averager[:], rhs=sums[:, g].rearrange("p f k -> p (f k)"),
                 start=True, stop=True,
             )
 
@@ -145,9 +132,7 @@ def tile_mlstmblock_pb_s_kernel(tc, h_attn, gn_w, gn_b, W_out, x, skip_scale, ou
         def v_var(g):
             for f in range(QUADS):
                 rows = slice(32 * f, 32 * (f + 1))
-                nc.vector.tensor_reduce(
-                    out=sel[rows, g], in_=means[g][rows, f], axis=mybir.AxisListType.X, op=ALU.add
-                )
+                nc.vector.tensor_copy(out=sel[rows, g], in_=means[g][rows, f])
             nc.vector.tensor_scalar(
                 out=negvar[:, g : g + 1], in0=sel[:, g, 0:1], scalar1=sel[:, g, 0:1], scalar2=sel[:, g, 1:2],
                 op0=ALU.mult, op1=ALU.subtract,
@@ -198,8 +183,8 @@ def tile_mlstmblock_pb_s_kernel(tc, h_attn, gn_w, gn_b, W_out, x, skip_scale, ou
         h_codes = data.tile([P, PASSES, S], U32, align_bytes=64)
         h_scales = data.tile([P, PASSES, S], U8, align_bytes=64)
 
-        def half_cols(half):
-            return slice(HALF * half, HALF * (half + 1))
+        def half_cols(part):
+            return (slice(0, 256), slice(256, 512), slice(256, 384), slice(384, 512))[part]
 
         def h_t_values(g, t):
             return h_t[g][t // 2][:].bitcast(BF16).rearrange("q (n e) -> q n e", e=2)[:, :, t % 2]
@@ -234,7 +219,7 @@ def tile_mlstmblock_pb_s_kernel(tc, h_attn, gn_w, gn_b, W_out, x, skip_scale, ou
         acc = {}
 
         def pe_mx(g, half):
-            for j in range(2 * half, 2 * half + 2):
+            for j in ((0, 1), (2, 3), (2,), (3,))[half]:
                 if g == 0:
                     acc[j] = psum.tile([P, DM], F32, tag=acc_bank[j], name="acc%d" % j)
                 nc.tensor.matmul_mx(
@@ -248,44 +233,47 @@ def tile_mlstmblock_pb_s_kernel(tc, h_attn, gn_w, gn_b, W_out, x, skip_scale, ou
                 )
 
         out_sb = data.tile([P, ROWS, DM], F32)
-        skip = const.tile([P, 1], F32)
-
-        def v_out(j):
-            nc.vector.scalar_tensor_tensor(
-                out=out_sb[:, j, :], in0=x_sb[:, j, :], scalar=skip[:, 0:1], in1=acc[j][:], op0=ALU.mult, op1=ALU.add
-            )
-            nc.sync.dma_start(out=out_rows[:, j, :], in_=out_sb[:, j, :])
+        def v_out(j, pieces=1):
+            width = DM // pieces
+            for i in range(pieces):
+                cols = slice(width * i, width * (i + 1))
+                nc.vector.scalar_tensor_tensor(
+                    out=out_sb[:, j, cols], in0=x_sb[:, j, cols], scalar=skip_bf[:, 0:1], in1=acc[j][:, cols],
+                    op0=ALU.mult, op1=ALU.add,
+                )
+                nc.sync.dma_start(out=out_rows[:, j, cols], in_=out_sb[:, j, cols])
 
         s_square(0, 0)
         v_bn(0, 1)
         s_square(0, 2)
         v_bn(0, 3)
         pe_sum(0, 0)
+        pe_sum(0, 1)
         pe_sum(0, 2)
+        pe_sum(0, 3)
         for u in range(2):
             nc.tensor.transpose(gn_t[:, u], gn_src[:].bitcast(F32)[:, u : 2 * P : 2], ident[:])
         v_copy_sums(0)
-        v_bn_post(0)
-        pe_h(0, 0)
         pe_means(0)
         s_square(1, 0)
-        pe_sum(1, 0)
-        s_square(1, 1)
-        pe_sum(1, 1)
+        v_bn(1, 1)
         s_square(1, 2)
-        pe_sum(1, 2)
+        s_square(1, 3)
         nc.vector.tensor_copy(
             out=gn_all[:].rearrange("q a g (u e) -> q (a g) u e", e=2),
             in_=gn_bank[:, 0 : 2 * P].bitcast(BF16).rearrange("q (u r e) -> q r u e", u=2, e=2)[:, 0:8],
         )
-        v_bn(1, 3)
+        pe_h(0, 0)
+        pe_sum(1, 0)
+        pe_sum(1, 1)
+        pe_sum(1, 2)
+        pe_sum(1, 3)
         pe_h(0, 1)
         v_var(0)
         s_rstd(0)
-        v_bn_post(1)
+        v_scale_shift(0)
         v_copy_sums(1)
         pe_means(1)
-        v_scale_shift(0)
         s_norm(0, 0, 0)
         s_norm(0, 0, 1)
         v_norm(0, 0, 2)
@@ -302,8 +290,8 @@ def tile_mlstmblock_pb_s_kernel(tc, h_attn, gn_w, gn_b, W_out, x, skip_scale, ou
         v_scale_shift(1)
         s_copy_w(0, 0)
         v_quant_h(0, 0)
-        v_group(0, 1)
         s_copy_w(0, 1)
+        v_group(0, 1)
         pe_h(1, 0)
         pe_h(1, 1)
         pe_w(1, 0)
@@ -312,9 +300,9 @@ def tile_mlstmblock_pb_s_kernel(tc, h_attn, gn_w, gn_b, W_out, x, skip_scale, ou
         s_norm(1, 0, 0)
         s_norm(1, 0, 1)
         v_quant_w(0)
+        v_norm(1, 0, 2)
+        v_norm(1, 0, 3)
         s_copy_w(1, 0)
-        s_norm(1, 0, 2)
-        s_norm(1, 0, 3)
         s_copy_w(1, 1)
         pe_mx(0, 0)
         pe_mx(0, 1)
@@ -323,11 +311,10 @@ def tile_mlstmblock_pb_s_kernel(tc, h_attn, gn_w, gn_b, W_out, x, skip_scale, ou
         s_norm(1, 1, 1)
         s_norm(1, 1, 2)
         s_norm(1, 1, 3)
-        v_quant_h(1, 0)
         v_quant_w(1)
+        v_quant_h(1, 0)
         pe_mx(1, 0)
         v_group(1, 1)
-        nc.vector.tensor_copy(out=skip[:], in_=skip_bf[:])
         v_out(0)
         v_quant_h(1, 1)
         pe_mx(1, 1)

@@ -71,6 +71,10 @@ def tile_mlstmblock_pb_s_kernel(tc, h_attn, gn_w, gn_b, W_out, x, skip_scale, ou
         make_identity(nc, ident[:])
         neg_ones = const.tile([P, 2], BF16)
         nc.vector.memset(neg_ones[:], -1.0)
+        own_head = const.tile([P, QUADS], F32)
+        nc.gpsimd.memset(own_head[:], 0.0)
+        for f in range(QUADS):
+            nc.gpsimd.memset(own_head[32 * f : 32 * (f + 1), f : f + 1], 1.0)
         averager = const.tile([P, P], F32)
         nc.vector.memset(averager[:], 1.0 / GROUP_SIZE)
 
@@ -88,8 +92,9 @@ def tile_mlstmblock_pb_s_kernel(tc, h_attn, gn_w, gn_b, W_out, x, skip_scale, ou
         sums = stat.tile([P, PASSES, QUADS, 2], F32)
         junk_s = stat.tile([P, 8, ROWS, HEAD_CH], BF16)
         junk_v = stat.tile([P, 8, ROWS, HEAD_CH], BF16)
-        sel = stat.tile([P, PASSES, 2], F32)
         gn_all = const.tile([P, 4, PASSES, 4], F32)
+        sel = stat.tile([P, PASSES, 2], F32)
+        junk_sel = stat.tile([P, PASSES, 2, QUADS], F32)
         negvar = stat.tile([P, PASSES], F32)
         rstd = stat.tile([P, PASSES], F32)
         ss = stat.tile([P, PASSES, 2, 4], F32)
@@ -130,9 +135,11 @@ def tile_mlstmblock_pb_s_kernel(tc, h_attn, gn_w, gn_b, W_out, x, skip_scale, ou
                 nc.tensor.transpose(h_t[g][u][:, P * j : P * (j + 1)], words[:, j, u : 2 * P : 2], ident[:])
 
         def v_var(g):
-            for f in range(QUADS):
-                rows = slice(32 * f, 32 * (f + 1))
-                nc.vector.tensor_copy(out=sel[rows, g], in_=means[g][rows, f])
+            for k in range(2):
+                nc.vector.scalar_tensor_tensor(
+                    out=junk_sel[:, g, k, :], in0=means[g][:, :, k], scalar=1.0, in1=own_head[:], op0=ALU.mult,
+                    op1=ALU.mult, accum_out=sel[:, g, k : k + 1],
+                )
             nc.vector.tensor_scalar(
                 out=negvar[:, g : g + 1], in0=sel[:, g, 0:1], scalar1=sel[:, g, 0:1], scalar2=sel[:, g, 1:2],
                 op0=ALU.mult, op1=ALU.subtract,
@@ -184,7 +191,7 @@ def tile_mlstmblock_pb_s_kernel(tc, h_attn, gn_w, gn_b, W_out, x, skip_scale, ou
         h_scales = data.tile([P, PASSES, S], U8, align_bytes=64)
 
         def half_cols(part):
-            return (slice(0, 256), slice(256, 512), slice(256, 384), slice(384, 512))[part]
+            return (slice(0, 256), slice(256, 512), slice(256, 384), slice(384, 512), slice(0, 512))[part]
 
         def h_t_values(g, t):
             return h_t[g][t // 2][:].bitcast(BF16).rearrange("q (n e) -> q n e", e=2)[:, :, t % 2]
@@ -219,7 +226,7 @@ def tile_mlstmblock_pb_s_kernel(tc, h_attn, gn_w, gn_b, W_out, x, skip_scale, ou
         acc = {}
 
         def pe_mx(g, half):
-            for j in ((0, 1), (2, 3), (2,), (3,))[half]:
+            for j in ((0, 1), (2, 3), (2,), (3,), (0, 1, 2, 3))[half]:
                 if g == 0:
                     acc[j] = psum.tile([P, DM], F32, tag=acc_bank[j], name="acc%d" % j)
                 nc.tensor.matmul_mx(

@@ -261,25 +261,25 @@ def tile_mlstmblock_pb_s_kernel(tc, h_attn, gn_w, gn_b, W_out, x, skip_scale, ou
         for u in range(2):
             nc.tensor.transpose(gn_t[:, u], gn_src[:].bitcast(F32)[:, u : 2 * P : 2], ident[:])
         v_copy_sums(0)
+        pe_sum(1, 0)
         pe_means(0)
         s_square(1, 0)
         v_bn(1, 1)
         s_square(1, 2)
-        s_square(1, 3)
         nc.vector.tensor_copy(
             out=gn_all[:].rearrange("q a g (u e) -> q (a g) u e", e=2),
             in_=gn_bank[:, 0 : 2 * P].bitcast(BF16).rearrange("q (u r e) -> q r u e", u=2, e=2)[:, 0:8],
         )
-        pe_h(0, 0)
-        pe_sum(1, 0)
         pe_sum(1, 1)
-        pe_sum(1, 2)
-        pe_sum(1, 3)
-        pe_h(0, 1)
+        pe_h(0, 0)
         v_var(0)
         s_rstd(0)
+        pe_sum(1, 2)
+        pe_sum(1, 3)
+        v_bn(1, 3)
         v_scale_shift(0)
         v_copy_sums(1)
+        pe_h(0, 1)
         pe_means(1)
         s_norm(0, 0, 0)
         s_norm(0, 0, 1)
@@ -287,32 +287,30 @@ def tile_mlstmblock_pb_s_kernel(tc, h_attn, gn_w, gn_b, W_out, x, skip_scale, ou
         v_norm(0, 0, 3)
         pe_w(0, 0)
         pe_w(0, 1)
-        v_var(1)
         s_norm(0, 1, 0)
         s_norm(0, 1, 1)
-        s_rstd(1)
+        v_var(1)
         s_norm(0, 1, 2)
         s_norm(0, 1, 3)
+        s_rstd(1)
         v_group(0, 0)
         v_scale_shift(1)
-        s_copy_w(0, 0)
-        v_quant_h(0, 0)
-        s_copy_w(0, 1)
         v_group(0, 1)
+        s_copy_w(0, 0)
+        v_quant_h(0, 4)
+        s_copy_w(0, 1)
         pe_h(1, 0)
         pe_h(1, 1)
         pe_w(1, 0)
         pe_w(1, 1)
-        v_quant_h(0, 1)
         s_norm(1, 0, 0)
         s_norm(1, 0, 1)
+        s_norm(1, 0, 2)
         v_quant_w(0)
-        v_norm(1, 0, 2)
         v_norm(1, 0, 3)
         s_copy_w(1, 0)
         s_copy_w(1, 1)
-        pe_mx(0, 0)
-        pe_mx(0, 1)
+        pe_mx(0, 4)
         v_group(1, 0)
         s_norm(1, 1, 0)
         s_norm(1, 1, 1)

from contextlib import ExitStack

import concourse.mybir as mybir
from concourse.masks import make_identity

FLOPS = 2 * 512 * 512 * 1024

BF16 = mybir.dt.bfloat16
F32 = mybir.dt.float32
U32 = mybir.dt.uint32
U8 = mybir.dt.uint8
FP8X4 = mybir.dt.float8_e4m3fn_x4
ALU = mybir.AluOpType
ACT = mybir.ActivationFunctionType

P = 128
S = 512
DM = 512
ROWS = S // P
PASSES = 2
PASS_CH = 512
QUADS = 4
HEAD_CH = 128
EPS_GN = 1e-5
GROUP_SIZE = S * HEAD_CH
HALF = S // 2


def tile_mlstmblock_pb_s_kernel(tc, h_attn, gn_w, gn_b, W_out, x, skip_scale, out):
    nc = tc.nc
    h_rows = h_attn.flatten_outer_dims().rearrange("(p j) k -> p j k", j=ROWS)
    x_rows = x.flatten_outer_dims().rearrange("(p j) m -> p j m", j=ROWS)
    out_rows = out.flatten_outer_dims().rearrange("(p j) m -> p j m", j=ROWS)
    w_rows = W_out.rearrange("(b p) k -> p b k", p=P)

    with ExitStack() as ctx:
        const = ctx.enter_context(tc.tile_pool(name="const", bufs=1))
        data = ctx.enter_context(tc.tile_pool(name="data", bufs=1))
        stat = ctx.enter_context(tc.tile_pool(name="stat", bufs=1))
        psum = ctx.enter_context(tc.psum_pool(name="psum", bufs=1))
        ctx.enter_context(tc.manual_schedule())

        gn_src = const.tile([P, PASS_CH], BF16)
        nc.vector.memset(gn_src[:], 0.0)
        hx = []
        for g in range(PASSES):
            hx_g = data.tile([P, ROWS, PASS_CH], BF16, name="hx%d" % g)
            hx.append(hx_g)
        for g in range(PASSES):
            for c in range(2):
                cols = slice(256 * c, 256 * (c + 1))
                nc.sync.dma_start(out=hx[g][:, :, cols], in_=h_rows[:, :, PASS_CH * g + 256 * c : PASS_CH * g + 256 * (c + 1)])
            if g == 0:
                nc.sync.dma_start(out=gn_src[0:2, :], in_=gn_w.rearrange("(g w) -> g w", g=PASSES))
                nc.sync.dma_start(out=gn_src[6:8, :], in_=gn_b.rearrange("(g w) -> g w", g=PASSES))
        w_sb = []
        for g in range(PASSES):
            w_g = data.tile([P, 4, PASS_CH], BF16, name="w_sb%d" % g)
            nc.sync.dma_start(out=w_g[:], in_=w_rows[:, :, PASS_CH * g : PASS_CH * (g + 1)])
            w_sb.append(w_g)
        x_sb = data.tile([P, ROWS, DM], BF16)
        nc.sync.dma_start(out=x_sb[:], in_=x_rows)
        skip_bf = const.tile([P, 1], BF16)
        nc.sync.dma_start(out=skip_bf[:], in_=skip_scale.partition_broadcast(P))

        warm = const.tile([P, 1], F32)
        nc.vector.memset(warm[:], 1.0)
        warm_out = const.tile([P, 1], F32)
        nc.scalar.activation(out=warm_out[:], in_=warm[:], func=ACT.Abs_reciprocal_sqrt)
        ident = const.tile([P, P], F32)
        make_identity(nc, ident[:])
        neg_ones = const.tile([P, 2], BF16)
        nc.vector.memset(neg_ones[:], -1.0)
        own_head = const.tile([P, QUADS], F32)
        nc.gpsimd.memset(own_head[:], 0.0)
        for f in range(QUADS):
            nc.gpsimd.memset(own_head[32 * f : 32 * (f + 1), f : f + 1], 1.0)
        averager = const.tile([P, P], F32)
        nc.vector.memset(averager[:], 1.0 / GROUP_SIZE)

        small = psum.tile([P, 512], F32, tag="small")
        gn_bank = psum.tile([P, 512], F32, tag="w1", name="gn_bank")
        gn_t = gn_bank[:, 0 : 2 * P].rearrange("q (u r) -> q u r", u=2)
        stat_bank = (small, psum.tile([P, 512], F32, tag="small1", name="small1"))
        means = [stat_bank[g][:, 32:40].rearrange("q (f k) -> q f k", f=QUADS) for g in range(PASSES)]

        h_t = [
            [psum.tile([P, S], F32, tag="h_t%d%d" % (g, u), name="h_t%d%d" % (g, u)) for u in range(2)]
            for g in range(PASSES)
        ]

        sums = stat.tile([P, PASSES, QUADS, 2], F32)
        junk_s = stat.tile([P, 8, ROWS, HEAD_CH], BF16)
        junk_v = stat.tile([P, 8, ROWS, HEAD_CH], BF16)
        gn_all = const.tile([P, 4, PASSES, 4], F32)
        sel = stat.tile([P, PASSES, 2], F32)
        junk_sel = stat.tile([P, PASSES, 2, QUADS], F32)
        negvar = stat.tile([P, PASSES], F32)
        rstd = stat.tile([P, PASSES], F32)
        ss = stat.tile([P, PASSES, 2, 4], F32)

        def head(g, f):
            return hx[g][:, :, HEAD_CH * f : HEAD_CH * (f + 1)]

        def pe_sum(g, f):
            for j in range(ROWS):
                nc.tensor.matmul(
                    out=stat_bank[g][:, f : f + 1], lhsT=head(g, f)[:, j, :], rhs=neg_ones[:, 0:1],
                    start=(j == 0), stop=(j == ROWS - 1),
                )

        def s_square(g, f):
            nc.scalar.activation(
                out=junk_s[:, 4 * g + f], in_=head(g, f), func=ACT.Square, accum_out=sums[:, g, f, 1:2]
            )

        def v_bn(g, f):
            nc.vector.scalar_tensor_tensor(
                out=junk_v[:, 4 * g + f], in0=head(g, f), scalar=1.0, in1=head(g, f), op0=ALU.mult, op1=ALU.mult,
                accum_out=sums[:, g, f, 1:2],
            )

        def v_copy_sums(g):
            nc.vector.tensor_copy(out=sums[:, g, :, 0], in_=stat_bank[g][:, 0:QUADS])

        def pe_means(g):
            nc.tensor.matmul(
                out=stat_bank[g][:, 32:40], lhsT=averager[:], rhs=sums[:, g].rearrange("p f k -> p (f k)"),
                start=True, stop=True,
            )

        def pe_h(g, u):
            words = hx[g][:].bitcast(F32)
            for j in range(ROWS):
                nc.tensor.transpose(h_t[g][u][:, P * j : P * (j + 1)], words[:, j, u : 2 * P : 2], ident[:])

        def v_var(g):
            for k in range(2):
                nc.vector.scalar_tensor_tensor(
                    out=junk_sel[:, g, k, :], in0=means[g][:, :, k], scalar=1.0, in1=own_head[:], op0=ALU.mult,
                    op1=ALU.mult, accum_out=sel[:, g, k : k + 1],
                )
            nc.vector.tensor_scalar(
                out=negvar[:, g : g + 1], in0=sel[:, g, 0:1], scalar1=sel[:, g, 0:1], scalar2=sel[:, g, 1:2],
                op0=ALU.mult, op1=ALU.subtract,
            )
            nc.vector.tensor_scalar(
                out=gn_all[:, 1, g, :], in0=gn_all[:, 0, g, :], scalar1=sel[:, g, 0:1], scalar2=None, op0=ALU.mult
            )

        def s_rstd(g):
            nc.scalar.activation(
                out=rstd[:, g : g + 1], in_=negvar[:, g : g + 1], func=ACT.Abs_reciprocal_sqrt, scale=-1.0, bias=EPS_GN
            )

        def v_scale_shift(g):
            nc.vector.scalar_tensor_tensor(
                out=ss[:, g], in0=gn_all[:, 0:2, g, :], scalar=rstd[:, g : g + 1], in1=gn_all[:, 2:4, g, :],
                op0=ALU.mult, op1=ALU.add,
            )

        w_grp = data.tile([P, PASSES, 4 * DM], BF16, align_bytes=64)
        w_words = w_grp[:].bitcast(F32).rearrange("q g (m u) -> q g m u", u=2)
        w_codes = data.tile([P, PASSES, DM], U32, align_bytes=64)
        w_scales = data.tile([P, PASSES, DM], U8, align_bytes=64)
        w_t = {}
        w_bank = (("w0", "w1"), ("small", "small1"))

        def pe_w(g, bp):
            w_t[(g, bp)] = psum.tile([P, 2, 256], F32, tag=w_bank[g][bp], name="w_t%d%d" % (g, bp))
            words = w_sb[g][:].bitcast(F32)
            for b in range(2):
                for u in range(2):
                    nc.tensor.transpose(
                        w_t[(g, bp)][:, u, P * b : P * (b + 1)], words[:, 2 * bp + b, u : 2 * P : 2], ident[:]
                    )

        def s_copy_w(g, bp):
            nc.scalar.copy(
                out=w_words[:, g, 256 * bp : 256 * (bp + 1), :], in_=w_t[(g, bp)][:].rearrange("q u m -> q m u")
            )

        def v_quant_w(g):
            nc.vector.quantize_mx(
                out=w_codes[:, g, :].bitcast(FP8X4), scales=w_scales[:, g, :], in_=w_grp[:, g, :]
            )

        h_norm = [data.tile([P, 4, S], BF16, name="h_norm%d" % g) for g in range(PASSES)]
        h_grp = [data.tile([P, S, 4], BF16, name="h_grp%d" % g, align_bytes=64) for g in range(PASSES)]
        h_codes = data.tile([P, PASSES, S], U32, align_bytes=64)
        h_scales = data.tile([P, PASSES, S], U8, align_bytes=64)

        def half_cols(part):
            return (slice(0, 256), slice(256, 512), slice(256, 384), slice(384, 512), slice(0, 512))[part]

        def h_t_values(g, t):
            return h_t[g][t // 2][:].bitcast(BF16).rearrange("q (n e) -> q n e", e=2)[:, :, t % 2]

        def s_norm(g, half, t):
            nc.scalar.activation(
                out=h_norm[g][:, t, half_cols(half)], in_=h_t_values(g, t)[:, half_cols(half)],
                func=ACT.Identity, scale=ss[:, g, 0, t : t + 1], bias=ss[:, g, 1, t : t + 1],
            )

        def v_norm(g, half, t):
            nc.vector.tensor_scalar(
                out=h_norm[g][:, t, half_cols(half)], in0=h_t_values(g, t)[:, half_cols(half)],
                scalar1=ss[:, g, 0, t : t + 1], scalar2=ss[:, g, 1, t : t + 1], op0=ALU.mult, op1=ALU.add,
            )

        def v_group(g, half):
            cols = half_cols(half)
            nc.vector.tensor_copy(
                out=h_grp[g][:, cols, :].rearrange("q (c i) t -> q c t i", i=4),
                in_=h_norm[g][:, :, cols].rearrange("q t (c i) -> q c t i", i=4),
            )

        def v_quant_h(g, half):
            cols = half_cols(half)
            nc.vector.quantize_mx(
                out=h_codes[:, g, cols].bitcast(FP8X4), scales=h_scales[:, g, cols],
                in_=h_grp[g][:, cols, :].rearrange("q n t -> q (n t)"),
            )

        acc_bank = ("w0", "w1", "small", "small1")
        acc = {}

        def pe_mx(g, half):
            for j in ((0, 1), (2, 3), (2,), (3,), (0, 1, 2, 3))[half]:
                if g == 0:
                    acc[j] = psum.tile([P, DM], F32, tag=acc_bank[j], name="acc%d" % j)
                nc.tensor.matmul_mx(
                    out=acc[j][:],
                    lhsT=h_codes[:, g, P * j : P * (j + 1)].bitcast(FP8X4),
                    lhsT_scale=h_scales[:, g, P * j : P * (j + 1)],
                    rhs=w_codes[:, g, :].bitcast(FP8X4),
                    rhs_scale=w_scales[:, g, :],
                    start=(g == 0),
                    stop=(g == PASSES - 1),
                )

        out_sb = data.tile([P, ROWS, DM], F32)
        def v_out(j, pieces=1):
            width = DM // pieces
            for i in range(pieces):
                cols = slice(width * i, width * (i + 1))
                nc.vector.scalar_tensor_tensor(
                    out=out_sb[:, j, cols], in0=x_sb[:, j, cols], scalar=skip_bf[:, 0:1], in1=acc[j][:, cols],
                    op0=ALU.mult, op1=ALU.add,
                )
                nc.sync.dma_start(out=out_rows[:, j, cols], in_=out_sb[:, j, cols])

        s_square(0, 0)
        v_bn(0, 1)
        s_square(0, 2)
        v_bn(0, 3)
        pe_sum(0, 0)
        pe_sum(0, 1)
        pe_sum(0, 2)
        pe_sum(0, 3)
        for u in range(2):
            nc.tensor.transpose(gn_t[:, u], gn_src[:].bitcast(F32)[:, u : 2 * P : 2], ident[:])
        v_copy_sums(0)
        pe_sum(1, 0)
        pe_means(0)
        s_square(1, 0)
        v_bn(1, 1)
        s_square(1, 2)
        nc.vector.tensor_copy(
            out=gn_all[:].rearrange("q a g (u e) -> q (a g) u e", e=2),
            in_=gn_bank[:, 0 : 2 * P].bitcast(BF16).rearrange("q (u r e) -> q r u e", u=2, e=2)[:, 0:8],
        )
        pe_sum(1, 1)
        pe_h(0, 0)
        v_var(0)
        s_rstd(0)
        pe_sum(1, 2)
        pe_sum(1, 3)
        v_bn(1, 3)
        v_scale_shift(0)
        v_copy_sums(1)
        pe_h(0, 1)
        pe_means(1)
        s_norm(0, 0, 0)
        s_norm(0, 0, 1)
        v_norm(0, 0, 2)
        v_norm(0, 0, 3)
        pe_w(0, 0)
        pe_w(0, 1)
        s_norm(0, 1, 0)
        s_norm(0, 1, 1)
        v_var(1)
        s_norm(0, 1, 2)
        s_norm(0, 1, 3)
        s_rstd(1)
        v_group(0, 0)
        v_scale_shift(1)
        v_group(0, 1)
        s_copy_w(0, 0)
        v_quant_h(0, 4)
        s_copy_w(0, 1)
        pe_h(1, 0)
        pe_h(1, 1)
        pe_w(1, 0)
        pe_w(1, 1)
        s_norm(1, 0, 0)
        s_norm(1, 0, 1)
        s_norm(1, 0, 2)
        v_quant_w(0)
        v_norm(1, 0, 3)
        s_copy_w(1, 0)
        s_copy_w(1, 1)
        pe_mx(0, 4)
        v_group(1, 0)
        s_norm(1, 1, 0)
        s_norm(1, 1, 1)
        s_norm(1, 1, 2)
        s_norm(1, 1, 3)
        v_quant_w(1)
        v_quant_h(1, 0)
        pe_mx(1, 0)
        v_group(1, 1)
        v_out(0)
        v_quant_h(1, 1)
        pe_mx(1, 1)
        v_out(1)
        v_out(2)
        v_out(3)
